import numpy as np
import ml_dtypes

BF16 = ml_dtypes.bfloat16


def bf(x):
    return np.asarray(x, np.float32).astype(BF16)


def f32(x):
    return np.asarray(x, np.float32)


def f64(x):
    return np.asarray(x).astype(np.float64)


def striped(idx):
    return np.tile(idx.reshape(-1, 16).T, (8, 1))


S, D, H, M, N = 512, 128, 64, 128, 1024
BASE = 10000.0


def build_cache():
    freqs = BASE ** (-np.arange(H) / H)
    angles = np.outer(np.arange(S), freqs)
    return np.stack([np.sin(angles), np.cos(angles)], axis=-1).reshape(S, D)


def setup_inputs():
    return {"table": bf(build_cache()), "w": bf(np.eye(D, M)[np.arange(D) ^ 1]), "offs": striped(np.random.permutation(np.tile(np.arange(S), 2))[:N])}


def reference(table, w, offs):
    idx = offs[:16].T.reshape(-1)
    return f64(w).T @ f64(table)[idx].T

@@ -1,0 +1,44 @@
+import concourse.mybir as mybir
+from concourse.masks import make_identity
+
+P = 128
+S, D, M, N = 512, 128, 128, 1024
+PIECE = 512
+FLOPS = 2 * D * M * N
+
+BF16, F32, U16 = mybir.dt.bfloat16, mybir.dt.float32, mybir.dt.uint16
+
+
+def tile_scalarropeembedding_kernel(tc, table, w, offs, out):
+    nc = tc.nc
+    with (
+        tc.tile_pool(name="held", bufs=1) as held,
+        tc.psum_pool(name="psum", bufs=1) as psum,
+    ):
+        offsets = held.tile([P, N // 16], U16, name="offsets")
+        nc.sync.dma_start(offsets[:], offs)
+
+        rows = held.tile([P, S // P, D], BF16, name="rows")
+        nc.sync.dma_start(rows[:], table.rearrange("(b p) d -> p b d", p=P))
+
+        weights = held.tile([D, M], BF16, name="weights")
+        nc.scalar.dma_start(weights[:], w)
+
+        identity = held.tile([P, P], BF16, name="identity")
+        make_identity(nc, identity[:])
+
+        flipped = psum.tile([D, S], BF16, name="flipped")
+        for b in range(S // P):
+            nc.tensor.transpose(flipped[:, b * P : (b + 1) * P], rows[:, b, :], identity[:])
+
+        window = held.tile([D, S], BF16, name="window")
+        nc.vector.tensor_copy(window[:], flipped[:])
+
+        for piece in range(N // PIECE):
+            columns = slice(piece * PIECE, (piece + 1) * PIECE)
+            entries = offsets[:, piece * (PIECE // 16) : (piece + 1) * (PIECE // 16)]
+            product = psum.tile([M, PIECE], F32, name=f"product{piece}")
+            nc.tensor.matmul(product[:], weights[:], window[:].indirect(entries), start=True, stop=True)
+            staged = held.tile([M, PIECE], F32, name=f"staged{piece}")
+            nc.vector.tensor_copy(staged[:], product[:])
+            nc.sync.dma_start(out[:, columns], staged[:])

@@ -3,7 +3,7 @@ from concourse.masks import make_identity
 
 P = 128
 S, D, M, N = 512, 128, 128, 1024
-PIECE = 512
+PIECE = 256
 FLOPS = 2 * D * M * N
 
 BF16, F32, U16 = mybir.dt.bfloat16, mybir.dt.float32, mybir.dt.uint16
@@ -40,5 +40,9 @@ def tile_scalarropeembedding_kernel(tc, table, w, offs, out):
             product = psum.tile([M, PIECE], F32, name=f"product{piece}")
             nc.tensor.matmul(product[:], weights[:], window[:].indirect(entries), start=True, stop=True)
             staged = held.tile([M, PIECE], F32, name=f"staged{piece}")
-            nc.vector.tensor_copy(staged[:], product[:])
-            nc.sync.dma_start(out[:, columns], staged[:])
+            if piece % 2 == 0:
+                nc.vector.tensor_copy(staged[:], product[:])
+                nc.sync.dma_start(out[:, columns], staged[:])
+            else:
+                nc.scalar.copy(staged[:], product[:])
+                nc.scalar.dma_start(out[:, columns], staged[:])

@@ -4,6 +4,8 @@ from concourse.masks import make_identity
 P = 128
 S, D, M, N = 512, 128, 128, 1024
 PIECE = 256
+BANK = 512
+WARMUP = 6
 FLOPS = 2 * D * M * N
 
 BF16, F32, U16 = mybir.dt.bfloat16, mybir.dt.float32, mybir.dt.uint16
@@ -26,6 +28,12 @@ def tile_scalarropeembedding_kernel(tc, table, w, offs, out):
 
         identity = held.tile([P, P], BF16, name="identity")
         make_identity(nc, identity[:])
+
+        zeros = held.tile([P, BANK], BF16, name="zeros")
+        nc.vector.memset(zeros[:], 0.0)
+        unread = psum.tile([P, BANK], F32, name="unread")
+        for turn in range(WARMUP):
+            nc.tensor.matmul(unread[:], zeros[:, :P], zeros[:], start=True, stop=True)
 
         flipped = psum.tile([D, S], BF16, name="flipped")
         for b in range(S // P):

@@ -4,8 +4,8 @@ from concourse.masks import make_identity
 P = 128
 S, D, M, N = 512, 128, 128, 1024
 PIECE = 256
-BANK = 512
-WARMUP = 6
+WARMUP = 16
+FILL = 4
 FLOPS = 2 * D * M * N
 
 BF16, F32, U16 = mybir.dt.bfloat16, mybir.dt.float32, mybir.dt.uint16
@@ -29,11 +29,11 @@ def tile_scalarropeembedding_kernel(tc, table, w, offs, out):
         identity = held.tile([P, P], BF16, name="identity")
         make_identity(nc, identity[:])
 
-        zeros = held.tile([P, BANK], BF16, name="zeros")
+        zeros = held.tile([P, P], BF16, name="zeros")
         nc.vector.memset(zeros[:], 0.0)
-        unread = psum.tile([P, BANK], F32, name="unread")
+        unread = psum.tile([P, P], F32, name="unread")
         for turn in range(WARMUP):
-            nc.tensor.matmul(unread[:], zeros[:, :P], zeros[:], start=True, stop=True)
+            nc.tensor.matmul(unread[:], zeros[:], zeros[:], start=True, stop=True)
 
         flipped = psum.tile([D, S], BF16, name="flipped")
         for b in range(S // P):
@@ -41,6 +41,9 @@ def tile_scalarropeembedding_kernel(tc, table, w, offs, out):
 
         window = held.tile([D, S], BF16, name="window")
         nc.vector.tensor_copy(window[:], flipped[:])
+
+        for turn in range(FILL):
+            nc.tensor.matmul(unread[:], zeros[:], zeros[:], start=True, stop=True)
 
         for piece in range(N // PIECE):
             columns = slice(piece * PIECE, (piece + 1) * PIECE)

@@ -5,7 +5,6 @@ P = 128
 S, D, M, N = 512, 128, 128, 1024
 PIECE = 256
 WARMUP = 16
-FILL = 4
 FLOPS = 2 * D * M * N
 
 BF16, F32, U16 = mybir.dt.bfloat16, mybir.dt.float32, mybir.dt.uint16
@@ -41,9 +40,6 @@ def tile_scalarropeembedding_kernel(tc, table, w, offs, out):
 
         window = held.tile([D, S], BF16, name="window")
         nc.vector.tensor_copy(window[:], flipped[:])
-
-        for turn in range(FILL):
-            nc.tensor.matmul(unread[:], zeros[:], zeros[:], start=True, stop=True)
 
         for piece in range(N // PIECE):
             columns = slice(piece * PIECE, (piece + 1) * PIECE)

@@ -16,11 +16,11 @@ def tile_scalarropeembedding_kernel(tc, table, w, offs, out):
         tc.tile_pool(name="held", bufs=1) as held,
         tc.psum_pool(name="psum", bufs=1) as psum,
     ):
-        offsets = held.tile([P, N // 16], U16, name="offsets")
-        nc.sync.dma_start(offsets[:], offs)
-
         rows = held.tile([P, S // P, D], BF16, name="rows")
         nc.sync.dma_start(rows[:], table.rearrange("(b p) d -> p b d", p=P))
+
+        offsets = held.tile([P, N // 16], U16, name="offsets")
+        nc.sync.dma_start(offsets[:], offs)
 
         weights = held.tile([D, M], BF16, name="weights")
         nc.scalar.dma_start(weights[:], w)

@@ -4,7 +4,7 @@ from concourse.masks import make_identity
 P = 128
 S, D, M, N = 512, 128, 128, 1024
 PIECE = 256
-WARMUP = 16
+WARMUP = 12
 FLOPS = 2 * D * M * N
 
 BF16, F32, U16 = mybir.dt.bfloat16, mybir.dt.float32, mybir.dt.uint16

@@ -16,8 +16,8 @@ def tile_scalarropeembedding_kernel(tc, table, w, offs, out):
         tc.tile_pool(name="held", bufs=1) as held,
         tc.psum_pool(name="psum", bufs=1) as psum,
     ):
-        rows = held.tile([P, S // P, D], BF16, name="rows")
-        nc.sync.dma_start(rows[:], table.rearrange("(b p) d -> p b d", p=P))
+        rows = held.tile([P, 2, 2, D], BF16, name="rows")
+        nc.sync.dma_start(rows[:], table.rearrange("(h p t) d -> p h t d", h=2, t=2))
 
         offsets = held.tile([P, N // 16], U16, name="offsets")
         nc.sync.dma_start(offsets[:], offs)
@@ -34,12 +34,15 @@ def tile_scalarropeembedding_kernel(tc, table, w, offs, out):
         for turn in range(WARMUP):
             nc.tensor.matmul(unread[:], zeros[:], zeros[:], start=True, stop=True)
 
-        flipped = psum.tile([D, S], BF16, name="flipped")
-        for b in range(S // P):
-            nc.tensor.transpose(flipped[:, b * P : (b + 1) * P], rows[:, b, :], identity[:])
-
         window = held.tile([D, S], BF16, name="window")
-        nc.vector.tensor_copy(window[:], flipped[:])
+        for h in range(2):
+            flipped = psum.tile([D, 2, P], BF16, name=f"flipped{h}")
+            for t in range(2):
+                nc.tensor.transpose(flipped[:, t, :], rows[:, h, t, :], identity[:])
+            nc.vector.tensor_copy(
+                window[:, h * 2 * P : (h + 1) * 2 * P].rearrange("d (p t) -> d p t", t=2),
+                flipped[:].rearrange("d t p -> d p t"),
+            )
 
         for piece in range(N // PIECE):
             columns = slice(piece * PIECE, (piece + 1) * PIECE)

@@ -16,8 +16,10 @@ def tile_scalarropeembedding_kernel(tc, table, w, offs, out):
         tc.tile_pool(name="held", bufs=1) as held,
         tc.psum_pool(name="psum", bufs=1) as psum,
     ):
-        rows = held.tile([P, 2, 2, D], BF16, name="rows")
-        nc.sync.dma_start(rows[:], table.rearrange("(h p t) d -> p h t d", h=2, t=2))
+        halves = table.rearrange("(h p t) d -> h p t d", h=2, t=2)
+        rows = [held.tile([P, 2, D], BF16, name=f"rows{h}") for h in range(2)]
+        nc.sync.dma_start(rows[0][:], halves[0, :, :, :])
+        nc.scalar.dma_start(rows[1][:], halves[1, :, :, :])
 
         offsets = held.tile([P, N // 16], U16, name="offsets")
         nc.sync.dma_start(offsets[:], offs)
@@ -38,7 +40,7 @@ def tile_scalarropeembedding_kernel(tc, table, w, offs, out):
         for h in range(2):
             flipped = psum.tile([D, 2, P], BF16, name=f"flipped{h}")
             for t in range(2):
-                nc.tensor.transpose(flipped[:, t, :], rows[:, h, t, :], identity[:])
+                nc.tensor.transpose(flipped[:, t, :], rows[h][:, t, :], identity[:])
             nc.vector.tensor_copy(
                 window[:, h * 2 * P : (h + 1) * 2 * P].rearrange("d (p t) -> d p t", t=2),
                 flipped[:].rearrange("d t p -> d p t"),

@@ -16,7 +16,7 @@ def tile_scalarropeembedding_kernel(tc, table, w, offs, out):
         tc.tile_pool(name="held", bufs=1) as held,
         tc.psum_pool(name="psum", bufs=1) as psum,
     ):
-        halves = table.rearrange("(h p t) d -> h p t d", h=2, t=2)
+        halves = table.rearrange("(h t p) d -> h p t d", h=2, t=2)
         rows = [held.tile([P, 2, D], BF16, name=f"rows{h}") for h in range(2)]
         nc.sync.dma_start(rows[0][:], halves[0, :, :, :])
         nc.scalar.dma_start(rows[1][:], halves[1, :, :, :])
@@ -42,8 +42,7 @@ def tile_scalarropeembedding_kernel(tc, table, w, offs, out):
             for t in range(2):
                 nc.tensor.transpose(flipped[:, t, :], rows[h][:, t, :], identity[:])
             nc.vector.tensor_copy(
-                window[:, h * 2 * P : (h + 1) * 2 * P].rearrange("d (p t) -> d p t", t=2),
-                flipped[:].rearrange("d t p -> d p t"),
+                window[:, h * 2 * P : (h + 1) * 2 * P].rearrange("d (t p) -> d t p", t=2), flipped[:]
             )
 
         for piece in range(N // PIECE):

@@ -4,7 +4,7 @@ from concourse.masks import make_identity
 P = 128
 S, D, M, N = 512, 128, 128, 1024
 PIECE = 256
-WARMUP = 12
+WARMUP = 8
 FLOPS = 2 * D * M * N
 
 BF16, F32, U16 = mybir.dt.bfloat16, mybir.dt.float32, mybir.dt.uint16
@@ -32,23 +32,21 @@ def tile_scalarropeembedding_kernel(tc, table, w, offs, out):
 
         zeros = held.tile([P, P], BF16, name="zeros")
         nc.vector.memset(zeros[:], 0.0)
-        unread = psum.tile([P, P], F32, name="unread")
+        products = [psum.tile([M, PIECE], F32, name=f"product{piece}") for piece in range(N // PIECE)]
         for turn in range(WARMUP):
-            nc.tensor.matmul(unread[:], zeros[:], zeros[:], start=True, stop=True)
+            nc.tensor.matmul(products[-1][:, :P], zeros[:], zeros[:], start=True, stop=True)
 
         window = held.tile([D, S], BF16, name="window")
-        for h in range(2):
-            flipped = psum.tile([D, 2, P], BF16, name=f"flipped{h}")
-            for t in range(2):
-                nc.tensor.transpose(flipped[:, t, :], rows[h][:, t, :], identity[:])
-            nc.vector.tensor_copy(
-                window[:, h * 2 * P : (h + 1) * 2 * P].rearrange("d (t p) -> d t p", t=2), flipped[:]
-            )
+        for block in range(S // P):
+            flipped = psum.tile([D, P], BF16, name=f"flipped{block}")
+            nc.tensor.transpose(flipped[:], rows[block // 2][:, block % 2, :], identity[:])
+            copy = nc.vector.tensor_copy if block % 2 == 0 else nc.scalar.copy
+            copy(window[:, block * P : (block + 1) * P], flipped[:])
 
         for piece in range(N // PIECE):
             columns = slice(piece * PIECE, (piece + 1) * PIECE)
             entries = offsets[:, piece * (PIECE // 16) : (piece + 1) * (PIECE // 16)]
-            product = psum.tile([M, PIECE], F32, name=f"product{piece}")
+            product = products[piece]
             nc.tensor.matmul(product[:], weights[:], window[:].indirect(entries), start=True, stop=True)
             staged = held.tile([M, PIECE], F32, name=f"staged{piece}")
             if piece % 2 == 0:

@@ -32,21 +32,23 @@ def tile_scalarropeembedding_kernel(tc, table, w, offs, out):
 
         zeros = held.tile([P, P], BF16, name="zeros")
         nc.vector.memset(zeros[:], 0.0)
-        products = [psum.tile([M, PIECE], F32, name=f"product{piece}") for piece in range(N // PIECE)]
+        unread = psum.tile([P, P], F32, name="unread")
         for turn in range(WARMUP):
-            nc.tensor.matmul(products[-1][:, :P], zeros[:], zeros[:], start=True, stop=True)
+            nc.tensor.matmul(unread[:], zeros[:], zeros[:], start=True, stop=True)
 
         window = held.tile([D, S], BF16, name="window")
-        for block in range(S // P):
-            flipped = psum.tile([D, P], BF16, name=f"flipped{block}")
-            nc.tensor.transpose(flipped[:], rows[block // 2][:, block % 2, :], identity[:])
-            copy = nc.vector.tensor_copy if block % 2 == 0 else nc.scalar.copy
-            copy(window[:, block * P : (block + 1) * P], flipped[:])
+        for h in range(2):
+            flipped = psum.tile([D, 2, P], BF16, name=f"flipped{h}")
+            for t in range(2):
+                nc.tensor.transpose(flipped[:, t, :], rows[h][:, t, :], identity[:])
+            nc.vector.tensor_copy(
+                window[:, h * 2 * P : (h + 1) * 2 * P].rearrange("d (t p) -> d t p", t=2), flipped[:]
+            )
 
         for piece in range(N // PIECE):
             columns = slice(piece * PIECE, (piece + 1) * PIECE)
             entries = offsets[:, piece * (PIECE // 16) : (piece + 1) * (PIECE // 16)]
-            product = products[piece]
+            product = psum.tile([M, PIECE], F32, name=f"product{piece}")
             nc.tensor.matmul(product[:], weights[:], window[:].indirect(entries), start=True, stop=True)
             staged = held.tile([M, PIECE], F32, name=f"staged{piece}")
             if piece % 2 == 0:

import concourse.mybir as mybir
from concourse.masks import make_identity

P = 128
S, D, M, N = 512, 128, 128, 1024
PIECE = 256
WARMUP = 8
FLOPS = 2 * D * M * N

BF16, F32, U16 = mybir.dt.bfloat16, mybir.dt.float32, mybir.dt.uint16


def tile_scalarropeembedding_kernel(tc, table, w, offs, out):
    nc = tc.nc
    with (
        tc.tile_pool(name="held", bufs=1) as held,
        tc.psum_pool(name="psum", bufs=1) as psum,
    ):
        halves = table.rearrange("(h t p) d -> h p t d", h=2, t=2)
        rows = [held.tile([P, 2, D], BF16, name=f"rows{h}") for h in range(2)]
        nc.sync.dma_start(rows[0][:], halves[0, :, :, :])
        nc.scalar.dma_start(rows[1][:], halves[1, :, :, :])

        offsets = held.tile([P, N // 16], U16, name="offsets")
        nc.sync.dma_start(offsets[:], offs)

        weights = held.tile([D, M], BF16, name="weights")
        nc.scalar.dma_start(weights[:], w)

        identity = held.tile([P, P], BF16, name="identity")
        make_identity(nc, identity[:])

        zeros = held.tile([P, P], BF16, name="zeros")
        nc.vector.memset(zeros[:], 0.0)
        unread = psum.tile([P, P], F32, name="unread")
        for turn in range(WARMUP):
            nc.tensor.matmul(unread[:], zeros[:], zeros[:], start=True, stop=True)

        window = held.tile([D, S], BF16, name="window")
        for h in range(2):
            flipped = psum.tile([D, 2, P], BF16, name=f"flipped{h}")
            for t in range(2):
                nc.tensor.transpose(flipped[:, t, :], rows[h][:, t, :], identity[:])
            nc.vector.tensor_copy(
                window[:, h * 2 * P : (h + 1) * 2 * P].rearrange("d (t p) -> d t p", t=2), flipped[:]
            )

        for piece in range(N // PIECE):
            columns = slice(piece * PIECE, (piece + 1) * PIECE)
            entries = offsets[:, piece * (PIECE // 16) : (piece + 1) * (PIECE // 16)]
            product = psum.tile([M, PIECE], F32, name=f"product{piece}")
            nc.tensor.matmul(product[:], weights[:], window[:].indirect(entries), start=True, stop=True)
            staged = held.tile([M, PIECE], F32, name=f"staged{piece}")
            if piece % 2 == 0:
                nc.vector.tensor_copy(staged[:], product[:])
                nc.sync.dma_start(out[:, columns], staged[:])
            else:
                nc.scalar.copy(staged[:], product[:])
                nc.scalar.dma_start(out[:, columns], staged[:])
